import numpy as np
import ml_dtypes


def mxq(x, axis, fmt="e4m3"):
    dtype, down = {"e4m3": (ml_dtypes.float8_e4m3fn, 7), "e5m2": (ml_dtypes.float8_e5m2, 14)}[fmt]
    v = np.moveaxis(np.asarray(x, np.float32).astype(ml_dtypes.bfloat16).astype(np.float64), axis, -1)
    blocks = v.reshape(v.shape[:-1] + (-1, 32))
    amax = np.abs(blocks).max(-1, keepdims=True)
    byte = np.maximum(np.where(amax > 0, np.frexp(amax)[1] - 1 + 127, 0) - down, 1)
    scale = np.exp2(byte - 127.0)
    codes = (blocks / scale).astype(np.float32).astype(dtype).astype(np.float64)
    return np.moveaxis((codes * scale).reshape(v.shape), -1, axis)


WIDE = False


def mx_kscale(k):
    if not WIDE:
        return np.ones(k)
    levels = np.array([10, -10, 5, -5, 0])
    if k % 512:
        return np.exp2(np.random.permutation(np.resize(levels, k // 32))).repeat(32)
    a = np.empty((k // 512, 16))
    for p in range(k // 512):
        a[p, :8] = np.random.permutation(np.resize(levels, 8))
        for g in range(8):
            far = levels[np.abs(levels - a[p, g]) >= 10]
            a[p, g + 8] = far[np.random.randint(len(far))]
    return np.exp2(a.ravel()).repeat(32)


BF16 = ml_dtypes.bfloat16


def bf(x):
    return np.asarray(x, np.float32).astype(BF16)


def f64(x):
    return np.asarray(x).astype(np.float64)


B, C, D, MIP, HH, WW = 8, 512, 256, 32, 32, 32
N = HH * WW


def sigmoid(v):
    return 1.0 / (1.0 + np.exp(-v))


def setup_inputs():
    s = mx_kscale(C)
    return {"x": bf(np.random.standard_normal((B, C, HH, WW)) * s[None, :, None, None]),
            "q_w": bf(np.random.standard_normal((D, C)) * 0.6 / np.sqrt(C) / s[None, :]),
            "q_b": bf(np.random.standard_normal(D) * 0.1),
            "k_w": bf(np.random.standard_normal((D, C)) * 0.6 / np.sqrt(C) / s[None, :]),
            "k_b": bf(np.random.standard_normal(D) * 0.1),
            "a_h": bf(sigmoid(np.random.standard_normal((B, D, HH))) / s[None, :D, None]),
            "a_w": bf(sigmoid(np.random.standard_normal((B, D, WW))))}


def reference(x, q_w, q_b, k_w, k_b, a_h, a_w):
    x4 = f64(x)
    xq = mxq(x4.reshape(B, C, N), 1, "e4m3")
    q = ((mxq(f64(q_w), 1, "e4m3") @ xq) + f64(q_b)[None, :, None]).transpose(0, 2, 1)
    k = (mxq(f64(k_w), 1, "e4m3") @ xq) + f64(k_b)[None, :, None]
    bias = (f64(a_w)[:, :, None, :] * f64(a_h)[:, :, :, None] * x4[:, :D]).reshape(B, D, N)
    return q, k + bias

@@ -1,0 +1,203 @@
+from contextlib import ExitStack
+
+import concourse.mybir as mybir
+from concourse.masks import make_identity
+
+F32 = mybir.dt.float32
+BF16 = mybir.dt.bfloat16
+U32 = mybir.dt.uint32
+U8 = mybir.dt.uint8
+FP8X4 = mybir.dt.float8_e4m3fn_x4
+ADD = mybir.AluOpType.add
+MULT = mybir.AluOpType.mult
+COPY = mybir.ActivationFunctionType.Copy
+
+B, C, D, HH, WW = 8, 512, 256, 32, 32
+N = HH * WW
+P = 128
+PACK = 4
+HALF = 512
+Q_TILES = HALF // P
+RUN = 4
+HALVES = N // HALF
+SCALAR_PIXELS = N // 2
+
+FLOPS = 2 * 2 * B * D * C * N
+
+
+def quantise_weight(nc, const, psum, ident, rows, label):
+    turned = psum.tile([P, 2, D], F32, tag="bank", name=label + "_turned")
+    for h in range(2):
+        words = rows[:, h, :].bitcast(F32)
+        for u in range(2):
+            nc.tensor.transpose(turned[:, u, h * P : (h + 1) * P], words[:, u : 2 * P : 2], ident[:])
+    grouped = const.tile([P, D * PACK], BF16, align_bytes=64, name=label + "_grouped")
+    nc.vector.tensor_copy(
+        out=grouped[:].bitcast(F32).rearrange("p (c u) -> p c u", u=2),
+        in_=turned[:].rearrange("p u c -> p c u"),
+    )
+    codes = const.tile([P, D], U32, align_bytes=64, name=label + "_codes")
+    scales = const.tile([P, D], U8, align_bytes=64, name=label + "_scales")
+    nc.vector.quantize_mx(out=codes[:].bitcast(FP8X4), scales=scales[:], in_=grouped[:])
+    return codes, scales
+
+
+def tile_self_attn_pa_t_kernel(tc, x, q_w, q_b, k_w, k_b, a_h, a_w, out_0, out_1):
+    nc = tc.nc
+    with ExitStack() as ctx:
+        const = ctx.enter_context(tc.tile_pool(name="const", bufs=1))
+        maps = ctx.enter_context(tc.tile_pool(name="maps", bufs=B))
+        work = ctx.enter_context(tc.tile_pool(name="work", bufs=2))
+        gates = ctx.enter_context(tc.tile_pool(name="gates", bufs=3))
+        results = ctx.enter_context(tc.tile_pool(name="results", bufs=3))
+        psum = ctx.enter_context(tc.psum_pool(name="psum", bufs=8))
+        ctx.enter_context(tc.manual_schedule())
+
+        x_tiles = [maps.tile([P, PACK, N], BF16, name="x_b") for b in range(B)]
+        xg_tiles = [maps.tile([P, 2, N], BF16, name="xg_b") for b in range(B)]
+        ah = const.tile([P, B, 2, HH], BF16)
+        aw = const.tile([P, B, 2, WW], BF16)
+
+        def load_map(b):
+            nc.sync.dma_start(out=ah[:, b], in_=a_h[b].rearrange("(p e) i -> p e i", e=2))
+            nc.sync.dma_start(out=aw[:, b], in_=a_w[b].rearrange("(p e) j -> p e j", e=2))
+            nc.sync.dma_start(
+                out=x_tiles[b][:].rearrange("p t n -> p (t n)"), in_=x[b].rearrange("(p t) i j -> p (t i j)", t=PACK)
+            )
+            nc.sync.dma_start(
+                out=xg_tiles[b][:].rearrange("p e n -> p (e n)"), in_=x[b, :D].rearrange("(p e) i j -> p (e i j)", e=2)
+            )
+
+        load_map(0)
+        kw_rows = const.tile([P, 2, C], BF16)
+        nc.sync.dma_start(out=kw_rows[:], in_=k_w.rearrange("(p e) c -> p e c", e=2))
+        qw_rows = const.tile([P, 2, C], BF16)
+        nc.sync.dma_start(out=qw_rows[:], in_=q_w.rearrange("(h p) c -> p h c", p=P))
+        for b in range(1, B):
+            load_map(b)
+        kb = const.tile([P, 2], BF16)
+        nc.scalar.dma_start(out=kb[:], in_=k_b.rearrange("(p e) -> p e", e=2))
+        qb = const.tile([P, D], BF16)
+        nc.scalar.dma_start(out=qb[:], in_=q_b.partition_broadcast(P))
+
+        ident = const.tile([P, P], F32)
+        make_identity(nc, ident[:])
+        ah_f32 = const.tile([P, B, 2, HH], F32)
+
+        grouped, gated, codes, scales, banks, q_sb, k_sb = {}, {}, {}, {}, {}, {}, {}
+
+        def gate_at_once(b):
+            gated[b] = gates.tile([P, 2, N], F32, name="gated")
+            nc.vector.tensor_tensor(
+                out=gated[b][:].rearrange("p e (i j) -> p e i j", j=WW),
+                in0=ah[:, b].unsqueeze(3).to_broadcast([P, 2, HH, WW]),
+                in1=aw[:, b].unsqueeze(2).to_broadcast([P, 2, HH, WW]),
+                op=MULT,
+            )
+
+        def gate_by_rows(b):
+            gated[b] = gates.tile([P, 2, N], F32, name="gated")
+            nc.scalar.copy(out=ah_f32[:, b], in_=ah[:, b])
+            for e in range(2):
+                for i in range(HH):
+                    nc.scalar.activation(
+                        out=gated[b][:, e, i * WW : (i + 1) * WW],
+                        in_=aw[:, b, e, :],
+                        func=COPY,
+                        scale=ah_f32[:, b, e, i : i + 1],
+                    )
+
+        def prepare(b):
+            x_b = x_tiles[b]
+            for g in range(HALVES):
+                pixels = slice(g * HALF, (g + 1) * HALF)
+                for e in range(2):
+                    nc.gpsimd.tensor_tensor(
+                        out=gated[b][:, e, pixels], in0=gated[b][:, e, pixels], in1=xg_tiles[b][:, e, pixels], op=MULT
+                    )
+            grouped[b] = work.tile([P, N, PACK], BF16, align_bytes=64, name="grouped")
+            nc.scalar.copy(
+                out=grouped[b][:, :SCALAR_PIXELS].rearrange("p (c i) t -> p c t i", i=RUN),
+                in_=x_b[:, :, :SCALAR_PIXELS].rearrange("p t (c i) -> p c t i", i=RUN),
+            )
+            nc.vector.tensor_copy(
+                out=grouped[b][:, SCALAR_PIXELS:].rearrange("p (c i) t -> p c t i", i=RUN),
+                in_=x_b[:, :, SCALAR_PIXELS:].rearrange("p t (c i) -> p c t i", i=RUN),
+            )
+
+        def quantise(b):
+            codes[b] = work.tile([P, N], U32, align_bytes=64, name="codes")
+            scales[b] = work.tile([P, N], U8, align_bytes=64, name="scales")
+            nc.vector.quantize_mx(
+                out=codes[b][:].bitcast(FP8X4), scales=scales[b][:], in_=grouped[b][:].rearrange("p n t -> p (n t)")
+            )
+
+        def project(b, g):
+            pixels = slice(g * HALF, (g + 1) * HALF)
+            banks[b, g] = []
+            for e in range(2):
+                k_acc = psum.tile([P, HALF], F32, tag="bank")
+                nc.tensor.matmul_mx(
+                    out=k_acc[:],
+                    lhsT=kw_codes[:, e * P : (e + 1) * P].bitcast(FP8X4),
+                    lhsT_scale=kw_scales[:, e * P : (e + 1) * P],
+                    rhs=codes[b][:, pixels].bitcast(FP8X4),
+                    rhs_scale=scales[b][:, pixels],
+                    start=True,
+                    stop=True,
+                )
+                banks[b, g].append(k_acc)
+            for pair in range(Q_TILES // 2):
+                q_acc = psum.tile([P, 2, D], F32, tag="bank")
+                for s in range(2):
+                    first = g * HALF + (2 * pair + s) * P
+                    nc.tensor.matmul_mx(
+                        out=q_acc[:, s, :],
+                        lhsT=codes[b][:, first : first + P].bitcast(FP8X4),
+                        lhsT_scale=scales[b][:, first : first + P],
+                        rhs=qw_codes[:].bitcast(FP8X4),
+                        rhs_scale=qw_scales[:],
+                        start=True,
+                        stop=True,
+                    )
+                banks[b, g].append(q_acc)
+
+        def finish(b, g):
+            pixels = slice(g * HALF, (g + 1) * HALF)
+            if g == 0:
+                q_sb[b] = results.tile([P, HALVES, Q_TILES, D], F32, name="q_sb")
+                k_sb[b] = results.tile([P, 2, N], F32, name="k_sb")
+            for e in range(2):
+                nc.vector.scalar_tensor_tensor(
+                    out=k_sb[b][:, e, pixels],
+                    in0=banks[b, g][e][:],
+                    scalar=kb[:, e : e + 1],
+                    in1=gated[b][:, e, pixels],
+                    op0=ADD,
+                    op1=ADD,
+                )
+            nc.sync.dma_start(
+                out=out_1[b].rearrange("(p e) n -> p e n", e=2)[:, :, pixels], in_=k_sb[b][:, :, pixels]
+            )
+            for pair in range(Q_TILES // 2):
+                nc.vector.tensor_tensor(
+                    out=q_sb[b][:, g, 2 * pair : 2 * pair + 2, :],
+                    in0=banks[b, g][2 + pair][:],
+                    in1=qb[:].unsqueeze(1).to_broadcast([P, 2, D]),
+                    op=ADD,
+                )
+            nc.sync.dma_start(out=out_0[b, pixels, :].rearrange("(s m) d -> m s d", m=P), in_=q_sb[b][:, g])
+
+        gate_at_once(0)
+        kw_codes, kw_scales = quantise_weight(nc, const, psum, ident, kw_rows, "kw")
+        qw_codes, qw_scales = quantise_weight(nc, const, psum, ident, qw_rows, "qw")
+        prepare(0)
+        for b in range(B):
+            quantise(b)
+            if b + 1 < B:
+                gate_by_rows(b + 1)
+                prepare(b + 1)
+            for g in range(HALVES):
+                project(b, g)
+            for g in range(HALVES):
+                finish(b, g)

@@ -58,9 +58,11 @@ def tile_self_attn_pa_t_kernel(tc, x, q_w, q_b, k_w, k_b, a_h, a_w, out_0, out_1
         ah = const.tile([P, B, 2, HH], BF16)
         aw = const.tile([P, B, 2, WW], BF16)
 
-        def load_map(b):
+        def load_gates(b):
             nc.sync.dma_start(out=ah[:, b], in_=a_h[b].rearrange("(p e) i -> p e i", e=2))
             nc.sync.dma_start(out=aw[:, b], in_=a_w[b].rearrange("(p e) j -> p e j", e=2))
+
+        def load_map(b):
             nc.sync.dma_start(
                 out=x_tiles[b][:].rearrange("p t n -> p (t n)"), in_=x[b].rearrange("(p t) i j -> p (t i j)", t=PACK)
             )
@@ -68,12 +70,14 @@ def tile_self_attn_pa_t_kernel(tc, x, q_w, q_b, k_w, k_b, a_h, a_w, out_0, out_1
                 out=xg_tiles[b][:].rearrange("p e n -> p (e n)"), in_=x[b, :D].rearrange("(p e) i j -> p (e i j)", e=2)
             )
 
-        load_map(0)
+        load_gates(0)
         kw_rows = const.tile([P, 2, C], BF16)
         nc.sync.dma_start(out=kw_rows[:], in_=k_w.rearrange("(p e) c -> p e c", e=2))
         qw_rows = const.tile([P, 2, C], BF16)
         nc.sync.dma_start(out=qw_rows[:], in_=q_w.rearrange("(h p) c -> p h c", p=P))
+        load_map(0)
         for b in range(1, B):
+            load_gates(b)
             load_map(b)
         kb = const.tile([P, 2], BF16)
         nc.scalar.dma_start(out=kb[:], in_=k_b.rearrange("(p e) -> p e", e=2))

@@ -20,7 +20,15 @@ HALF = 512
 Q_TILES = HALF // P
 RUN = 4
 HALVES = N // HALF
-SCALAR_PIXELS = N // 2
+
+
+def scalar_pixels(b):
+    if b == 0:
+        return N // 4
+    if b == B - 1:
+        return N
+    return N // 2
+
 
 FLOPS = 2 * 2 * B * D * C * N
 
@@ -32,7 +40,7 @@ def quantise_weight(nc, const, psum, ident, rows, label):
         for u in range(2):
             nc.tensor.transpose(turned[:, u, h * P : (h + 1) * P], words[:, u : 2 * P : 2], ident[:])
     grouped = const.tile([P, D * PACK], BF16, align_bytes=64, name=label + "_grouped")
-    nc.vector.tensor_copy(
+    nc.scalar.copy(
         out=grouped[:].bitcast(F32).rearrange("p (c u) -> p c u", u=2),
         in_=turned[:].rearrange("p u c -> p c u"),
     )
@@ -49,7 +57,7 @@ def tile_self_attn_pa_t_kernel(tc, x, q_w, q_b, k_w, k_b, a_h, a_w, out_0, out_1
         maps = ctx.enter_context(tc.tile_pool(name="maps", bufs=B))
         work = ctx.enter_context(tc.tile_pool(name="work", bufs=2))
         gates = ctx.enter_context(tc.tile_pool(name="gates", bufs=3))
-        results = ctx.enter_context(tc.tile_pool(name="results", bufs=3))
+        results = ctx.enter_context(tc.tile_pool(name="results", bufs=4))
         psum = ctx.enter_context(tc.psum_pool(name="psum", bufs=8))
         ctx.enter_context(tc.manual_schedule())
 
@@ -81,8 +89,11 @@ def tile_self_attn_pa_t_kernel(tc, x, q_w, q_b, k_w, k_b, a_h, a_w, out_0, out_1
             load_map(b)
         kb = const.tile([P, 2], BF16)
         nc.scalar.dma_start(out=kb[:], in_=k_b.rearrange("(p e) -> p e", e=2))
-        qb = const.tile([P, D], BF16)
-        nc.scalar.dma_start(out=qb[:], in_=q_b.partition_broadcast(P))
+        qb_row = const.tile([P, D], BF16)
+        nc.vector.memset(qb_row[:], 0.0)
+        nc.scalar.dma_start(out=qb_row[0:1, :], in_=q_b.rearrange("(o d) -> o d", o=1))
+        ones = const.tile([P, P], BF16)
+        nc.vector.memset(ones[:], 1.0)
 
         ident = const.tile([P, P], F32)
         make_identity(nc, ident[:])
@@ -120,21 +131,29 @@ def tile_self_attn_pa_t_kernel(tc, x, q_w, q_b, k_w, k_b, a_h, a_w, out_0, out_1
                         out=gated[b][:, e, pixels], in0=gated[b][:, e, pixels], in1=xg_tiles[b][:, e, pixels], op=MULT
                     )
             grouped[b] = work.tile([P, N, PACK], BF16, align_bytes=64, name="grouped")
-            nc.scalar.copy(
-                out=grouped[b][:, :SCALAR_PIXELS].rearrange("p (c i) t -> p c t i", i=RUN),
-                in_=x_b[:, :, :SCALAR_PIXELS].rearrange("p t (c i) -> p c t i", i=RUN),
-            )
-            nc.vector.tensor_copy(
-                out=grouped[b][:, SCALAR_PIXELS:].rearrange("p (c i) t -> p c t i", i=RUN),
-                in_=x_b[:, :, SCALAR_PIXELS:].rearrange("p t (c i) -> p c t i", i=RUN),
-            )
+            split = scalar_pixels(b)
+            for first in range(0, split, HALF):
+                last = min(first + HALF, split)
+                nc.scalar.copy(
+                    out=grouped[b][:, first:last].rearrange("p (c i) t -> p c t i", i=RUN),
+                    in_=x_b[:, :, first:last].rearrange("p t (c i) -> p c t i", i=RUN),
+                )
+            if split < N:
+                nc.vector.tensor_copy(
+                    out=grouped[b][:, split:].rearrange("p (c i) t -> p c t i", i=RUN),
+                    in_=x_b[:, :, split:].rearrange("p t (c i) -> p c t i", i=RUN),
+                )
 
         def quantise(b):
             codes[b] = work.tile([P, N], U32, align_bytes=64, name="codes")
             scales[b] = work.tile([P, N], U8, align_bytes=64, name="scales")
-            nc.vector.quantize_mx(
-                out=codes[b][:].bitcast(FP8X4), scales=scales[b][:], in_=grouped[b][:].rearrange("p n t -> p (n t)")
-            )
+            width = N if b + 1 < B and scalar_pixels(b + 1) < N else HALF
+            for first in range(0, N, width):
+                nc.vector.quantize_mx(
+                    out=codes[b][:, first : first + width].bitcast(FP8X4),
+                    scales=scales[b][:, first : first + width],
+                    in_=grouped[b][:, first : first + width].rearrange("p n t -> p (n t)"),
+                )
 
         def project(b, g):
             pixels = slice(g * HALF, (g + 1) * HALF)
@@ -195,9 +214,14 @@ def tile_self_attn_pa_t_kernel(tc, x, q_w, q_b, k_w, k_b, a_h, a_w, out_0, out_1
         gate_at_once(0)
         kw_codes, kw_scales = quantise_weight(nc, const, psum, ident, kw_rows, "kw")
         qw_codes, qw_scales = quantise_weight(nc, const, psum, ident, qw_rows, "qw")
+        qb_bank = psum.tile([P, HALF], F32, tag="bank")
+        nc.tensor.matmul(out=qb_bank[:, :D], lhsT=ones[:], rhs=qb_row[:], start=True, stop=True)
+        qb = const.tile([P, D], BF16)
         prepare(0)
         for b in range(B):
             quantise(b)
+            if b == 0:
+                nc.vector.tensor_copy(out=qb[:], in_=qb_bank[:, :D])
             if b + 1 < B:
                 gate_by_rows(b + 1)
                 prepare(b + 1)

@@ -22,12 +22,12 @@ RUN = 4
 HALVES = N // HALF
 
 
-def scalar_pixels(b):
+def shares(b):
     if b == 0:
-        return N // 4
+        return (("S", 0, P), ("V", P, HALF), ("S", HALF, HALF + P), ("V", HALF + P, N))
     if b == B - 1:
-        return N
-    return N // 2
+        return (("S", 0, HALF), ("S", HALF, N))
+    return (("S", 0, HALF), ("V", HALF, N))
 
 
 FLOPS = 2 * 2 * B * D * C * N
@@ -54,26 +54,31 @@ def tile_self_attn_pa_t_kernel(tc, x, q_w, q_b, k_w, k_b, a_h, a_w, out_0, out_1
     nc = tc.nc
     with ExitStack() as ctx:
         const = ctx.enter_context(tc.tile_pool(name="const", bufs=1))
-        maps = ctx.enter_context(tc.tile_pool(name="maps", bufs=B))
+        maps = ctx.enter_context(tc.tile_pool(name="maps", bufs=B - 1))
+        copies = ctx.enter_context(tc.tile_pool(name="copies", bufs=B))
         work = ctx.enter_context(tc.tile_pool(name="work", bufs=2))
         gates = ctx.enter_context(tc.tile_pool(name="gates", bufs=3))
         results = ctx.enter_context(tc.tile_pool(name="results", bufs=4))
         psum = ctx.enter_context(tc.psum_pool(name="psum", bufs=8))
         ctx.enter_context(tc.manual_schedule())
 
-        x_tiles = [maps.tile([P, PACK, N], BF16, name="x_b") for b in range(B)]
-        xg_tiles = [maps.tile([P, 2, N], BF16, name="xg_b") for b in range(B)]
+        x_first = [const.tile([P, PACK, HALF], BF16, name="x_first_%d" % g) for g in range(HALVES)]
+        x_tiles = [None] + [maps.tile([P, PACK, N], BF16, name="x_b") for b in range(1, B)]
+        xg_tiles = [copies.tile([P, 2, N], BF16, name="xg_b") for b in range(B)]
         ah = const.tile([P, B, 2, HH], BF16)
         aw = const.tile([P, B, 2, WW], BF16)
+
+        def x_rows(b, first, last):
+            if b > 0:
+                return x_tiles[b][:, :, first:last]
+            g = first // HALF
+            return x_first[g][:, :, first - g * HALF : last - g * HALF]
 
         def load_gates(b):
             nc.sync.dma_start(out=ah[:, b], in_=a_h[b].rearrange("(p e) i -> p e i", e=2))
             nc.sync.dma_start(out=aw[:, b], in_=a_w[b].rearrange("(p e) j -> p e j", e=2))
 
-        def load_map(b):
-            nc.sync.dma_start(
-                out=x_tiles[b][:].rearrange("p t n -> p (t n)"), in_=x[b].rearrange("(p t) i j -> p (t i j)", t=PACK)
-            )
+        def load_copy(b):
             nc.sync.dma_start(
                 out=xg_tiles[b][:].rearrange("p e n -> p (e n)"), in_=x[b, :D].rearrange("(p e) i j -> p (e i j)", e=2)
             )
@@ -83,10 +88,17 @@ def tile_self_attn_pa_t_kernel(tc, x, q_w, q_b, k_w, k_b, a_h, a_w, out_0, out_1
         nc.sync.dma_start(out=kw_rows[:], in_=k_w.rearrange("(p e) c -> p e c", e=2))
         qw_rows = const.tile([P, 2, C], BF16)
         nc.sync.dma_start(out=qw_rows[:], in_=q_w.rearrange("(h p) c -> p h c", p=P))
-        load_map(0)
+        for g in range(HALVES):
+            nc.sync.dma_start(
+                out=x_first[g][:], in_=x[0].rearrange("(p t) i j -> p t (i j)", t=PACK)[:, :, g * HALF : (g + 1) * HALF]
+            )
+        load_copy(0)
         for b in range(1, B):
             load_gates(b)
-            load_map(b)
+            nc.sync.dma_start(
+                out=x_tiles[b][:].rearrange("p t n -> p (t n)"), in_=x[b].rearrange("(p t) i j -> p (t i j)", t=PACK)
+            )
+            load_copy(b)
         kb = const.tile([P, 2], BF16)
         nc.scalar.dma_start(out=kb[:], in_=k_b.rearrange("(p e) -> p e", e=2))
         qb_row = const.tile([P, D], BF16)
@@ -122,54 +134,41 @@ def tile_self_attn_pa_t_kernel(tc, x, q_w, q_b, k_w, k_b, a_h, a_w, out_0, out_1
                         scale=ah_f32[:, b, e, i : i + 1],
                     )
 
-        def prepare(b):
-            x_b = x_tiles[b]
+        def gate_times_x(b):
             for g in range(HALVES):
                 pixels = slice(g * HALF, (g + 1) * HALF)
                 for e in range(2):
                     nc.gpsimd.tensor_tensor(
                         out=gated[b][:, e, pixels], in0=gated[b][:, e, pixels], in1=xg_tiles[b][:, e, pixels], op=MULT
                     )
-            grouped[b] = work.tile([P, N, PACK], BF16, align_bytes=64, name="grouped")
-            split = scalar_pixels(b)
-            for first in range(0, split, HALF):
-                last = min(first + HALF, split)
-                nc.scalar.copy(
-                    out=grouped[b][:, first:last].rearrange("p (c i) t -> p c t i", i=RUN),
-                    in_=x_b[:, :, first:last].rearrange("p t (c i) -> p c t i", i=RUN),
-                )
-            if split < N:
-                nc.vector.tensor_copy(
-                    out=grouped[b][:, split:].rearrange("p (c i) t -> p c t i", i=RUN),
-                    in_=x_b[:, :, split:].rearrange("p t (c i) -> p c t i", i=RUN),
-                )
 
-        def quantise(b):
-            codes[b] = work.tile([P, N], U32, align_bytes=64, name="codes")
-            scales[b] = work.tile([P, N], U8, align_bytes=64, name="scales")
-            width = N if b + 1 < B and scalar_pixels(b + 1) < N else HALF
-            for first in range(0, N, width):
-                nc.vector.quantize_mx(
-                    out=codes[b][:, first : first + width].bitcast(FP8X4),
-                    scales=scales[b][:, first : first + width],
-                    in_=grouped[b][:, first : first + width].rearrange("p n t -> p (n t)"),
-                )
+        def regroup(b, who, halves=(0, 1)):
+            if b not in grouped:
+                grouped[b] = work.tile([P, N, PACK], BF16, align_bytes=64, name="grouped")
+            for engine, first, last in shares(b):
+                g = first // HALF
+                if engine == who and g in halves:
+                    m_first, m_last = (first - g * HALF) // RUN, (last - g * HALF) // RUN
+                    half = grouped[b][:, g * HALF : (g + 1) * HALF].rearrange("p (s m) t -> p m t s", s=RUN)
+                    out = half[:, m_first:m_last]
+                    in_ = x_rows(b, first, last).rearrange("p t (m s) -> p m t s", s=RUN)
+                    if who == "S":
+                        nc.scalar.copy(out=out, in_=in_)
+                    else:
+                        nc.vector.tensor_copy(out=out, in_=in_)
+
+        def quantise(b, first, last):
+            if b not in codes:
+                codes[b] = work.tile([P, N], U32, align_bytes=64, name="codes")
+                scales[b] = work.tile([P, N], U8, align_bytes=64, name="scales")
+            nc.vector.quantize_mx(
+                out=codes[b][:, first:last].bitcast(FP8X4),
+                scales=scales[b][:, first:last],
+                in_=grouped[b][:, first:last].rearrange("p n t -> p (n t)"),
+            )
 
         def project(b, g):
             pixels = slice(g * HALF, (g + 1) * HALF)
-            banks[b, g] = []
-            for e in range(2):
-                k_acc = psum.tile([P, HALF], F32, tag="bank")
-                nc.tensor.matmul_mx(
-                    out=k_acc[:],
-                    lhsT=kw_codes[:, e * P : (e + 1) * P].bitcast(FP8X4),
-                    lhsT_scale=kw_scales[:, e * P : (e + 1) * P],
-                    rhs=codes[b][:, pixels].bitcast(FP8X4),
-                    rhs_scale=scales[b][:, pixels],
-                    start=True,
-                    stop=True,
-                )
-                banks[b, g].append(k_acc)
             for pair in range(Q_TILES // 2):
                 q_acc = psum.tile([P, 2, D], F32, tag="bank")
                 for s in range(2):
@@ -183,49 +182,85 @@ def tile_self_attn_pa_t_kernel(tc, x, q_w, q_b, k_w, k_b, a_h, a_w, out_0, out_1
                         start=True,
                         stop=True,
                     )
-                banks[b, g].append(q_acc)
+                banks[b, g, "q", pair] = q_acc
+            for e in range(2):
+                k_acc = psum.tile([P, HALF], F32, tag="bank")
+                nc.tensor.matmul_mx(
+                    out=k_acc[:],
+                    lhsT=kw_codes[:, e * P : (e + 1) * P].bitcast(FP8X4),
+                    lhsT_scale=kw_scales[:, e * P : (e + 1) * P],
+                    rhs=codes[b][:, pixels].bitcast(FP8X4),
+                    rhs_scale=scales[b][:, pixels],
+                    start=True,
+                    stop=True,
+                )
+                banks[b, g, "k", e] = k_acc
 
         def finish(b, g):
             pixels = slice(g * HALF, (g + 1) * HALF)
+            last_of_all = b == B - 1 and g == HALVES - 1
             if g == 0:
                 q_sb[b] = results.tile([P, HALVES, Q_TILES, D], F32, name="q_sb")
                 k_sb[b] = results.tile([P, 2, N], F32, name="k_sb")
-            for e in range(2):
-                nc.vector.scalar_tensor_tensor(
-                    out=k_sb[b][:, e, pixels],
-                    in0=banks[b, g][e][:],
-                    scalar=kb[:, e : e + 1],
-                    in1=gated[b][:, e, pixels],
-                    op0=ADD,
-                    op1=ADD,
-                )
-            nc.sync.dma_start(
-                out=out_1[b].rearrange("(p e) n -> p e n", e=2)[:, :, pixels], in_=k_sb[b][:, :, pixels]
-            )
+            q_rows = out_0[b, pixels, :].rearrange("(m s) d -> m s d", s=RUN)
             for pair in range(Q_TILES // 2):
                 nc.vector.tensor_tensor(
                     out=q_sb[b][:, g, 2 * pair : 2 * pair + 2, :],
-                    in0=banks[b, g][2 + pair][:],
+                    in0=banks[b, g, "q", pair][:],
                     in1=qb[:].unsqueeze(1).to_broadcast([P, 2, D]),
                     op=ADD,
                 )
-            nc.sync.dma_start(out=out_0[b, pixels, :].rearrange("(s m) d -> m s d", m=P), in_=q_sb[b][:, g])
+                if last_of_all:
+                    nc.sync.dma_start(out=q_rows[:, 2 * pair : 2 * pair + 2, :], in_=q_sb[b][:, g, 2 * pair : 2 * pair + 2, :])
+            if not last_of_all:
+                nc.sync.dma_start(out=q_rows, in_=q_sb[b][:, g])
+            k_rows = out_1[b].rearrange("(p e) n -> p e n", e=2)[:, :, pixels]
+            for e in range(2):
+                nc.vector.scalar_tensor_tensor(
+                    out=k_sb[b][:, e, pixels].rearrange("p (m s) -> p m s", s=RUN),
+                    in0=banks[b, g, "k", e][:].rearrange("p (s m) -> p m s", s=RUN),
+                    scalar=kb[:, e : e + 1],
+                    in1=gated[b][:, e, pixels].rearrange("p (m s) -> p m s", s=RUN),
+                    op0=ADD,
+                    op1=ADD,
+                )
+                if b == B - 1:
+                    nc.sync.dma_start(out=k_rows[:, e, :], in_=k_sb[b][:, e, pixels])
+            if b < B - 1 and g == HALVES - 1:
+                nc.sync.dma_start(
+                    out=out_1[b].rearrange("(p e) n -> p (e n)", e=2), in_=k_sb[b][:].rearrange("p e n -> p (e n)")
+                )
 
         gate_at_once(0)
         kw_codes, kw_scales = quantise_weight(nc, const, psum, ident, kw_rows, "kw")
+        regroup(0, "S", (0,))
+        regroup(0, "V", (0,))
         qw_codes, qw_scales = quantise_weight(nc, const, psum, ident, qw_rows, "qw")
         qb_bank = psum.tile([P, HALF], F32, tag="bank")
         nc.tensor.matmul(out=qb_bank[:, :D], lhsT=ones[:], rhs=qb_row[:], start=True, stop=True)
         qb = const.tile([P, D], BF16)
-        prepare(0)
+        gate_times_x(0)
+        quantise(0, 0, HALF)
+        regroup(0, "S", (1,))
+        regroup(0, "V", (1,))
+        quantise(0, HALF, N)
+        nc.vector.tensor_copy(out=qb[:], in_=qb_bank[:, :D])
+
         for b in range(B):
-            quantise(b)
-            if b == 0:
-                nc.vector.tensor_copy(out=qb[:], in_=qb_bank[:, :D])
+            filler = b + 1 < B and any(engine == "V" for engine, first, last in shares(b + 1))
+            if b > 0:
+                width = N if filler else HALF
+                for first in range(0, N, width):
+                    quantise(b, first, first + width)
             if b + 1 < B:
                 gate_by_rows(b + 1)
-                prepare(b + 1)
+                gate_times_x(b + 1)
+                regroup(b + 1, "S")
+                if b > 0:
+                    regroup(b + 1, "V")
             for g in range(HALVES):
                 project(b, g)
-            for g in range(HALVES):
-                finish(b, g)
+            finish(b, 0)
+            if b == 0:
+                regroup(1, "V")
+            finish(b, 1)

@@ -22,13 +22,14 @@ RUN = 4
 HALVES = N // HALF
 
 
-def shares(b):
-    if b == 0:
-        return (("S", 0, P), ("V", P, HALF), ("S", HALF, HALF + P), ("V", HALF + P, N))
-    if b == B - 1:
-        return (("S", 0, HALF), ("S", HALF, N))
-    return (("S", 0, HALF), ("V", HALF, N))
+FIRST_SHARES = (("S", 0, P), ("V", P, HALF), ("S", HALF, HALF + P), ("V", HALF + P, N))
 
+
+def shares(b):
+    return (("S", 0, 0, RUN), ("S", 1, 0, 1), ("V", 1, 1, RUN)) if b % 2 == 0 else (("S", 0, 0, RUN), ("V", 1, 0, RUN))
+
+
+BY_PRODUCTS = (3, 6)
 
 FLOPS = 2 * 2 * B * D * C * N
 
@@ -98,7 +99,8 @@ def tile_self_attn_pa_t_kernel(tc, x, q_w, q_b, k_w, k_b, a_h, a_w, out_0, out_1
             nc.sync.dma_start(
                 out=x_tiles[b][:].rearrange("p t n -> p (t n)"), in_=x[b].rearrange("(p t) i j -> p (t i j)", t=PACK)
             )
-            load_copy(b)
+            if b not in BY_PRODUCTS:
+                load_copy(b)
         kb = const.tile([P, 2], BF16)
         nc.scalar.dma_start(out=kb[:], in_=k_b.rearrange("(p e) -> p e", e=2))
         qb_row = const.tile([P, D], BF16)
@@ -109,6 +111,10 @@ def tile_self_attn_pa_t_kernel(tc, x, q_w, q_b, k_w, k_b, a_h, a_w, out_0, out_1
 
         ident = const.tile([P, P], F32)
         make_identity(nc, ident[:])
+        spread = const.tile([P, 2, P], BF16)
+        nc.gpsimd.memset(spread[:], 0.0)
+        for u in range(2):
+            nc.gpsimd.tensor_copy(out=spread[:, u].rearrange("p (c v) -> p v c", v=2)[:, u], in_=ident[:, : P // 2])
         ah_f32 = const.tile([P, B, 2, HH], F32)
 
         grouped, gated, codes, scales, banks, q_sb, k_sb = {}, {}, {}, {}, {}, {}, {}
@@ -142,10 +148,33 @@ def tile_self_attn_pa_t_kernel(tc, x, q_w, q_b, k_w, k_b, a_h, a_w, out_0, out_1
                         out=gated[b][:, e, pixels], in0=gated[b][:, e, pixels], in1=xg_tiles[b][:, e, pixels], op=MULT
                     )
 
+        def spread_copy(b):
+            for e in range(2):
+                bank = psum.tile([P, HALVES, HALF], BF16, tag="bank", name="spread_bank")
+                for g in range(HALVES):
+                    for u in range(2):
+                        nc.tensor.matmul(
+                            out=bank[:, g],
+                            lhsT=spread[:, u],
+                            rhs=x_rows(b, g * HALF, (g + 1) * HALF)[:, 2 * u + e],
+                            start=u == 0,
+                            stop=u == 1,
+                        )
+                nc.scalar.copy(out=xg_tiles[b][:, e], in_=bank[:].rearrange("p g n -> p (g n)"))
+
         def regroup(b, who, halves=(0, 1)):
             if b not in grouped:
                 grouped[b] = work.tile([P, N, PACK], BF16, align_bytes=64, name="grouped")
-            for engine, first, last in shares(b):
+            for engine, g, s_first, s_last in shares(b) if b > 0 else ():
+                if engine == who:
+                    half = grouped[b][:, g * HALF : (g + 1) * HALF].rearrange("p (s m) t -> p m t s", s=RUN)
+                    out = half[:, :, :, s_first:s_last]
+                    in_ = x_rows(b, g * HALF, (g + 1) * HALF).rearrange("p t (m s) -> p m t s", s=RUN)[:, :, :, s_first:s_last]
+                    if who == "S":
+                        nc.scalar.copy(out=out, in_=in_)
+                    else:
+                        nc.vector.tensor_copy(out=out, in_=in_)
+            for engine, first, last in FIRST_SHARES if b == 0 else ():
                 g = first // HALF
                 if engine == who and g in halves:
                     m_first, m_last = (first - g * HALF) // RUN, (last - g * HALF) // RUN
@@ -224,9 +253,9 @@ def tile_self_attn_pa_t_kernel(tc, x, q_w, q_b, k_w, k_b, a_h, a_w, out_0, out_1
                     op0=ADD,
                     op1=ADD,
                 )
-                if b == B - 1:
+                if b >= B - 2:
                     nc.sync.dma_start(out=k_rows[:, e, :], in_=k_sb[b][:, e, pixels])
-            if b < B - 1 and g == HALVES - 1:
+            if b < B - 2 and g == HALVES - 1:
                 nc.sync.dma_start(
                     out=out_1[b].rearrange("(p e) n -> p (e n)", e=2), in_=k_sb[b][:].rearrange("p e n -> p (e n)")
                 )
@@ -247,15 +276,17 @@ def tile_self_attn_pa_t_kernel(tc, x, q_w, q_b, k_w, k_b, a_h, a_w, out_0, out_1
         nc.vector.tensor_copy(out=qb[:], in_=qb_bank[:, :D])
 
         for b in range(B):
-            filler = b + 1 < B and any(engine == "V" for engine, first, last in shares(b + 1))
+            filler = b + 1 < B
             if b > 0:
                 width = N if filler else HALF
                 for first in range(0, N, width):
                     quantise(b, first, first + width)
             if b + 1 < B:
+                regroup(b + 1, "S")
+                if b + 1 in BY_PRODUCTS:
+                    spread_copy(b + 1)
                 gate_by_rows(b + 1)
                 gate_times_x(b + 1)
-                regroup(b + 1, "S")
                 if b > 0:
                     regroup(b + 1, "V")
             for g in range(HALVES):

@@ -26,7 +26,7 @@ FIRST_SHARES = (("S", 0, P), ("V", P, HALF), ("S", HALF, HALF + P), ("V", HALF +
 
 
 def shares(b):
-    return (("S", 0, 0, RUN), ("S", 1, 0, 1), ("V", 1, 1, RUN)) if b % 2 == 0 else (("S", 0, 0, RUN), ("V", 1, 0, RUN))
+    return (("S", 0, 0, RUN), ("V", 1, 0, RUN))
 
 
 BY_PRODUCTS = (3, 6)
@@ -253,9 +253,9 @@ def tile_self_attn_pa_t_kernel(tc, x, q_w, q_b, k_w, k_b, a_h, a_w, out_0, out_1
                     op0=ADD,
                     op1=ADD,
                 )
-                if b >= B - 2:
+                if b == B - 1:
                     nc.sync.dma_start(out=k_rows[:, e, :], in_=k_sb[b][:, e, pixels])
-            if b < B - 2 and g == HALVES - 1:
+            if b < B - 1 and g == HALVES - 1:
                 nc.sync.dma_start(
                     out=out_1[b].rearrange("(p e) n -> p (e n)", e=2), in_=k_sb[b][:].rearrange("p e n -> p (e n)")
                 )
@@ -273,7 +273,7 @@ def tile_self_attn_pa_t_kernel(tc, x, q_w, q_b, k_w, k_b, a_h, a_w, out_0, out_1
         regroup(0, "S", (1,))
         regroup(0, "V", (1,))
         quantise(0, HALF, N)
-        nc.vector.tensor_copy(out=qb[:], in_=qb_bank[:, :D])
+        nc.scalar.copy(out=qb[:], in_=qb_bank[:, :D])
 
         for b in range(B):
             filler = b + 1 < B

@@ -26,10 +26,10 @@ FIRST_SHARES = (("S", 0, P), ("V", P, HALF), ("S", HALF, HALF + P), ("V", HALF +
 
 
 def shares(b):
-    return (("S", 0, 0, RUN), ("V", 1, 0, RUN))
+    return (("S", 0, 0, RUN), ("S", 1, 0, 2), ("V", 1, 2, RUN)) if b == B - 1 else (("S", 0, 0, RUN), ("V", 1, 0, RUN)) if b % 2 == 0 else (("S", 0, 0, RUN), ("S", 1, 0, 1), ("V", 1, 1, RUN))
 
 
-BY_PRODUCTS = (3, 6)
+BY_PRODUCTS = (4,)
 
 FLOPS = 2 * 2 * B * D * C * N
 

from contextlib import ExitStack

import concourse.mybir as mybir
from concourse.masks import make_identity

F32 = mybir.dt.float32
BF16 = mybir.dt.bfloat16
U32 = mybir.dt.uint32
U8 = mybir.dt.uint8
FP8X4 = mybir.dt.float8_e4m3fn_x4
ADD = mybir.AluOpType.add
MULT = mybir.AluOpType.mult
COPY = mybir.ActivationFunctionType.Copy

B, C, D, HH, WW = 8, 512, 256, 32, 32
N = HH * WW
P = 128
PACK = 4
HALF = 512
Q_TILES = HALF // P
RUN = 4
HALVES = N // HALF


FIRST_SHARES = (("S", 0, P), ("V", P, HALF), ("S", HALF, HALF + P), ("V", HALF + P, N))


def shares(b):
    return (("S", 0, 0, RUN), ("S", 1, 0, 2), ("V", 1, 2, RUN)) if b == B - 1 else (("S", 0, 0, RUN), ("V", 1, 0, RUN)) if b % 2 == 0 else (("S", 0, 0, RUN), ("S", 1, 0, 1), ("V", 1, 1, RUN))


BY_PRODUCTS = (4,)

FLOPS = 2 * 2 * B * D * C * N


def quantise_weight(nc, const, psum, ident, rows, label):
    turned = psum.tile([P, 2, D], F32, tag="bank", name=label + "_turned")
    for h in range(2):
        words = rows[:, h, :].bitcast(F32)
        for u in range(2):
            nc.tensor.transpose(turned[:, u, h * P : (h + 1) * P], words[:, u : 2 * P : 2], ident[:])
    grouped = const.tile([P, D * PACK], BF16, align_bytes=64, name=label + "_grouped")
    nc.scalar.copy(
        out=grouped[:].bitcast(F32).rearrange("p (c u) -> p c u", u=2),
        in_=turned[:].rearrange("p u c -> p c u"),
    )
    codes = const.tile([P, D], U32, align_bytes=64, name=label + "_codes")
    scales = const.tile([P, D], U8, align_bytes=64, name=label + "_scales")
    nc.vector.quantize_mx(out=codes[:].bitcast(FP8X4), scales=scales[:], in_=grouped[:])
    return codes, scales


def tile_self_attn_pa_t_kernel(tc, x, q_w, q_b, k_w, k_b, a_h, a_w, out_0, out_1):
    nc = tc.nc
    with ExitStack() as ctx:
        const = ctx.enter_context(tc.tile_pool(name="const", bufs=1))
        maps = ctx.enter_context(tc.tile_pool(name="maps", bufs=B - 1))
        copies = ctx.enter_context(tc.tile_pool(name="copies", bufs=B))
        work = ctx.enter_context(tc.tile_pool(name="work", bufs=2))
        gates = ctx.enter_context(tc.tile_pool(name="gates", bufs=3))
        results = ctx.enter_context(tc.tile_pool(name="results", bufs=4))
        psum = ctx.enter_context(tc.psum_pool(name="psum", bufs=8))
        ctx.enter_context(tc.manual_schedule())

        x_first = [const.tile([P, PACK, HALF], BF16, name="x_first_%d" % g) for g in range(HALVES)]
        x_tiles = [None] + [maps.tile([P, PACK, N], BF16, name="x_b") for b in range(1, B)]
        xg_tiles = [copies.tile([P, 2, N], BF16, name="xg_b") for b in range(B)]
        ah = const.tile([P, B, 2, HH], BF16)
        aw = const.tile([P, B, 2, WW], BF16)

        def x_rows(b, first, last):
            if b > 0:
                return x_tiles[b][:, :, first:last]
            g = first // HALF
            return x_first[g][:, :, first - g * HALF : last - g * HALF]

        def load_gates(b):
            nc.sync.dma_start(out=ah[:, b], in_=a_h[b].rearrange("(p e) i -> p e i", e=2))
            nc.sync.dma_start(out=aw[:, b], in_=a_w[b].rearrange("(p e) j -> p e j", e=2))

        def load_copy(b):
            nc.sync.dma_start(
                out=xg_tiles[b][:].rearrange("p e n -> p (e n)"), in_=x[b, :D].rearrange("(p e) i j -> p (e i j)", e=2)
            )

        load_gates(0)
        kw_rows = const.tile([P, 2, C], BF16)
        nc.sync.dma_start(out=kw_rows[:], in_=k_w.rearrange("(p e) c -> p e c", e=2))
        qw_rows = const.tile([P, 2, C], BF16)
        nc.sync.dma_start(out=qw_rows[:], in_=q_w.rearrange("(h p) c -> p h c", p=P))
        for g in range(HALVES):
            nc.sync.dma_start(
                out=x_first[g][:], in_=x[0].rearrange("(p t) i j -> p t (i j)", t=PACK)[:, :, g * HALF : (g + 1) * HALF]
            )
        load_copy(0)
        for b in range(1, B):
            load_gates(b)
            nc.sync.dma_start(
                out=x_tiles[b][:].rearrange("p t n -> p (t n)"), in_=x[b].rearrange("(p t) i j -> p (t i j)", t=PACK)
            )
            if b not in BY_PRODUCTS:
                load_copy(b)
        kb = const.tile([P, 2], BF16)
        nc.scalar.dma_start(out=kb[:], in_=k_b.rearrange("(p e) -> p e", e=2))
        qb_row = const.tile([P, D], BF16)
        nc.vector.memset(qb_row[:], 0.0)
        nc.scalar.dma_start(out=qb_row[0:1, :], in_=q_b.rearrange("(o d) -> o d", o=1))
        ones = const.tile([P, P], BF16)
        nc.vector.memset(ones[:], 1.0)

        ident = const.tile([P, P], F32)
        make_identity(nc, ident[:])
        spread = const.tile([P, 2, P], BF16)
        nc.gpsimd.memset(spread[:], 0.0)
        for u in range(2):
            nc.gpsimd.tensor_copy(out=spread[:, u].rearrange("p (c v) -> p v c", v=2)[:, u], in_=ident[:, : P // 2])
        ah_f32 = const.tile([P, B, 2, HH], F32)

        grouped, gated, codes, scales, banks, q_sb, k_sb = {}, {}, {}, {}, {}, {}, {}

        def gate_at_once(b):
            gated[b] = gates.tile([P, 2, N], F32, name="gated")
            nc.vector.tensor_tensor(
                out=gated[b][:].rearrange("p e (i j) -> p e i j", j=WW),
                in0=ah[:, b].unsqueeze(3).to_broadcast([P, 2, HH, WW]),
                in1=aw[:, b].unsqueeze(2).to_broadcast([P, 2, HH, WW]),
                op=MULT,
            )

        def gate_by_rows(b):
            gated[b] = gates.tile([P, 2, N], F32, name="gated")
            nc.scalar.copy(out=ah_f32[:, b], in_=ah[:, b])
            for e in range(2):
                for i in range(HH):
                    nc.scalar.activation(
                        out=gated[b][:, e, i * WW : (i + 1) * WW],
                        in_=aw[:, b, e, :],
                        func=COPY,
                        scale=ah_f32[:, b, e, i : i + 1],
                    )

        def gate_times_x(b):
            for g in range(HALVES):
                pixels = slice(g * HALF, (g + 1) * HALF)
                for e in range(2):
                    nc.gpsimd.tensor_tensor(
                        out=gated[b][:, e, pixels], in0=gated[b][:, e, pixels], in1=xg_tiles[b][:, e, pixels], op=MULT
                    )

        def spread_copy(b):
            for e in range(2):
                bank = psum.tile([P, HALVES, HALF], BF16, tag="bank", name="spread_bank")
                for g in range(HALVES):
                    for u in range(2):
                        nc.tensor.matmul(
                            out=bank[:, g],
                            lhsT=spread[:, u],
                            rhs=x_rows(b, g * HALF, (g + 1) * HALF)[:, 2 * u + e],
                            start=u == 0,
                            stop=u == 1,
                        )
                nc.scalar.copy(out=xg_tiles[b][:, e], in_=bank[:].rearrange("p g n -> p (g n)"))

        def regroup(b, who, halves=(0, 1)):
            if b not in grouped:
                grouped[b] = work.tile([P, N, PACK], BF16, align_bytes=64, name="grouped")
            for engine, g, s_first, s_last in shares(b) if b > 0 else ():
                if engine == who:
                    half = grouped[b][:, g * HALF : (g + 1) * HALF].rearrange("p (s m) t -> p m t s", s=RUN)
                    out = half[:, :, :, s_first:s_last]
                    in_ = x_rows(b, g * HALF, (g + 1) * HALF).rearrange("p t (m s) -> p m t s", s=RUN)[:, :, :, s_first:s_last]
                    if who == "S":
                        nc.scalar.copy(out=out, in_=in_)
                    else:
                        nc.vector.tensor_copy(out=out, in_=in_)
            for engine, first, last in FIRST_SHARES if b == 0 else ():
                g = first // HALF
                if engine == who and g in halves:
                    m_first, m_last = (first - g * HALF) // RUN, (last - g * HALF) // RUN
                    half = grouped[b][:, g * HALF : (g + 1) * HALF].rearrange("p (s m) t -> p m t s", s=RUN)
                    out = half[:, m_first:m_last]
                    in_ = x_rows(b, first, last).rearrange("p t (m s) -> p m t s", s=RUN)
                    if who == "S":
                        nc.scalar.copy(out=out, in_=in_)
                    else:
                        nc.vector.tensor_copy(out=out, in_=in_)

        def quantise(b, first, last):
            if b not in codes:
                codes[b] = work.tile([P, N], U32, align_bytes=64, name="codes")
                scales[b] = work.tile([P, N], U8, align_bytes=64, name="scales")
            nc.vector.quantize_mx(
                out=codes[b][:, first:last].bitcast(FP8X4),
                scales=scales[b][:, first:last],
                in_=grouped[b][:, first:last].rearrange("p n t -> p (n t)"),
            )

        def project(b, g):
            pixels = slice(g * HALF, (g + 1) * HALF)
            for pair in range(Q_TILES // 2):
                q_acc = psum.tile([P, 2, D], F32, tag="bank")
                for s in range(2):
                    first = g * HALF + (2 * pair + s) * P
                    nc.tensor.matmul_mx(
                        out=q_acc[:, s, :],
                        lhsT=codes[b][:, first : first + P].bitcast(FP8X4),
                        lhsT_scale=scales[b][:, first : first + P],
                        rhs=qw_codes[:].bitcast(FP8X4),
                        rhs_scale=qw_scales[:],
                        start=True,
                        stop=True,
                    )
                banks[b, g, "q", pair] = q_acc
            for e in range(2):
                k_acc = psum.tile([P, HALF], F32, tag="bank")
                nc.tensor.matmul_mx(
                    out=k_acc[:],
                    lhsT=kw_codes[:, e * P : (e + 1) * P].bitcast(FP8X4),
                    lhsT_scale=kw_scales[:, e * P : (e + 1) * P],
                    rhs=codes[b][:, pixels].bitcast(FP8X4),
                    rhs_scale=scales[b][:, pixels],
                    start=True,
                    stop=True,
                )
                banks[b, g, "k", e] = k_acc

        def finish(b, g):
            pixels = slice(g * HALF, (g + 1) * HALF)
            last_of_all = b == B - 1 and g == HALVES - 1
            if g == 0:
                q_sb[b] = results.tile([P, HALVES, Q_TILES, D], F32, name="q_sb")
                k_sb[b] = results.tile([P, 2, N], F32, name="k_sb")
            q_rows = out_0[b, pixels, :].rearrange("(m s) d -> m s d", s=RUN)
            for pair in range(Q_TILES // 2):
                nc.vector.tensor_tensor(
                    out=q_sb[b][:, g, 2 * pair : 2 * pair + 2, :],
                    in0=banks[b, g, "q", pair][:],
                    in1=qb[:].unsqueeze(1).to_broadcast([P, 2, D]),
                    op=ADD,
                )
                if last_of_all:
                    nc.sync.dma_start(out=q_rows[:, 2 * pair : 2 * pair + 2, :], in_=q_sb[b][:, g, 2 * pair : 2 * pair + 2, :])
            if not last_of_all:
                nc.sync.dma_start(out=q_rows, in_=q_sb[b][:, g])
            k_rows = out_1[b].rearrange("(p e) n -> p e n", e=2)[:, :, pixels]
            for e in range(2):
                nc.vector.scalar_tensor_tensor(
                    out=k_sb[b][:, e, pixels].rearrange("p (m s) -> p m s", s=RUN),
                    in0=banks[b, g, "k", e][:].rearrange("p (s m) -> p m s", s=RUN),
                    scalar=kb[:, e : e + 1],
                    in1=gated[b][:, e, pixels].rearrange("p (m s) -> p m s", s=RUN),
                    op0=ADD,
                    op1=ADD,
                )
                if b == B - 1:
                    nc.sync.dma_start(out=k_rows[:, e, :], in_=k_sb[b][:, e, pixels])
            if b < B - 1 and g == HALVES - 1:
                nc.sync.dma_start(
                    out=out_1[b].rearrange("(p e) n -> p (e n)", e=2), in_=k_sb[b][:].rearrange("p e n -> p (e n)")
                )

        gate_at_once(0)
        kw_codes, kw_scales = quantise_weight(nc, const, psum, ident, kw_rows, "kw")
        regroup(0, "S", (0,))
        regroup(0, "V", (0,))
        qw_codes, qw_scales = quantise_weight(nc, const, psum, ident, qw_rows, "qw")
        qb_bank = psum.tile([P, HALF], F32, tag="bank")
        nc.tensor.matmul(out=qb_bank[:, :D], lhsT=ones[:], rhs=qb_row[:], start=True, stop=True)
        qb = const.tile([P, D], BF16)
        gate_times_x(0)
        quantise(0, 0, HALF)
        regroup(0, "S", (1,))
        regroup(0, "V", (1,))
        quantise(0, HALF, N)
        nc.scalar.copy(out=qb[:], in_=qb_bank[:, :D])

        for b in range(B):
            filler = b + 1 < B
            if b > 0:
                width = N if filler else HALF
                for first in range(0, N, width):
                    quantise(b, first, first + width)
            if b + 1 < B:
                regroup(b + 1, "S")
                if b + 1 in BY_PRODUCTS:
                    spread_copy(b + 1)
                gate_by_rows(b + 1)
                gate_times_x(b + 1)
                if b > 0:
                    regroup(b + 1, "V")
            for g in range(HALVES):
                project(b, g)
            finish(b, 0)
            if b == 0:
                regroup(1, "V")
            finish(b, 1)
